import numpy as np
import ml_dtypes

BF16 = ml_dtypes.bfloat16


def bf(x):
    return np.asarray(x, np.float32).astype(BF16)


def f32(x):
    return np.asarray(x, np.float32)


def f64(x):
    return np.asarray(x).astype(np.float64)


def striped(idx):
    return np.tile(idx.reshape(-1, 16).T, (8, 1))


F, M, S, K, H, R, N = 128, 128, 1024, 8, 512, 16, 8192
EPS = 1e-5


def setup_inputs():
    return {
        "x": bf(np.random.standard_normal((F, S))),
        "w1": bf(np.random.standard_normal((F, M)) / np.sqrt(F)),
        "b1": f32(0.1 * np.random.standard_normal((M, 1))),
        "w2": bf(np.random.standard_normal((F, M)) * np.sqrt(K / F)),
        "b2": f32(0.1 * np.random.standard_normal((M, 1))),
        "gain": f32(1.0 + 0.1 * np.random.standard_normal((M, 1))),
        "shift": f32(0.1 * np.random.standard_normal((M, 1))),
        "offs": striped(np.concatenate([np.random.permutation(S)[:H] for _ in range(R)])),
    }


def reference(x, w1, b1, w2, b2, gain, shift, offs):
    idx = offs[:16].T.reshape(-1)
    xs = f64(x)
    near = (f64(w2).T @ xs[:, idx]).reshape(M, K, S).sum(axis=1) / K
    z = f64(w1).T @ xs + f64(b1) + near + f64(b2)
    r = np.maximum(z, 0.0)
    mu = r.mean(axis=1, keepdims=True)
    var = np.square(r - mu).mean(axis=1, keepdims=True)
    return (r - mu) / np.sqrt(var + EPS) * f64(gain) + f64(shift)

@@ -1,0 +1,91 @@
+import concourse.mybir as mybir
+
+BF16, F32, U16 = mybir.dt.bfloat16, mybir.dt.float32, mybir.dt.uint16
+ACT = mybir.ActivationFunctionType
+ALU = mybir.AluOpType
+
+P = 128
+NODES = 1024
+NEIGHBOURS = 8
+HALF = 512
+HALVES = NODES // HALF
+LIST_COLUMNS = HALF // 16
+EPS = 1e-5
+BN_STATS_DIM = 6
+
+FLOPS = 2 * P * P * NODES * (1 + NEIGHBOURS)
+
+
+def tile_resgcnnet_kernel(tc, x, w1, b1, w2, b2, gain, shift, offs, out):
+    nc = tc.nc
+    with (
+        tc.tile_pool(name="held", bufs=1) as held,
+        tc.psum_pool(name="psum", bufs=1) as psum,
+    ):
+        offsets = held.tile([P, NEIGHBOURS * NODES // 16], U16, name="offsets")
+        nc.sync.dma_start(offsets[:], offs)
+        nodes = held.tile([P, NODES], BF16, name="nodes")
+        nc.scalar.dma_start(nodes[:], x)
+        w1_sb = held.tile([P, P], BF16, name="w1_sb")
+        nc.scalar.dma_start(w1_sb[:], w1)
+        w2_sb = held.tile([P, P], BF16, name="w2_sb")
+        nc.sync.dma_start(w2_sb[:], w2)
+        b1_sb = held.tile([P, 1], F32, name="b1_sb")
+        nc.sync.dma_start(b1_sb[:], b1)
+        b2_sb = held.tile([P, 1], F32, name="b2_sb")
+        nc.sync.dma_start(b2_sb[:], b2)
+        gain_sb = held.tile([P, 1], F32, name="gain_sb")
+        nc.scalar.dma_start(gain_sb[:], gain)
+        shift_sb = held.tile([P, 1], F32, name="shift_sb")
+        nc.scalar.dma_start(shift_sb[:], shift)
+
+        w2_mean = held.tile([P, P], BF16, name="w2_mean")
+        nc.vector.tensor_scalar_mul(w2_mean[:], w2_sb[:], 1.0 / NEIGHBOURS)
+        bias = held.tile([P, 1], F32, name="bias")
+        nc.vector.tensor_add(bias[:], b1_sb[:], b2_sb[:])
+        eps = held.tile([P, 1], F32, name="eps")
+        nc.vector.memset(eps[:], EPS)
+
+        banks = [psum.tile([P, HALF], F32, name=f"bank{h}") for h in range(HALVES)]
+        for h in range(HALVES):
+            nc.tensor.matmul(
+                banks[h][:], w1_sb[:], nodes[:, h * HALF : (h + 1) * HALF], start=True, stop=False
+            )
+
+        r = held.tile([P, NODES], F32, name="r")
+        stats = held.tile([P, HALVES * BN_STATS_DIM], F32, name="stats")
+        for h in range(HALVES):
+            for t in range(NEIGHBOURS):
+                piece = HALVES * t + h
+                looked_up = nodes[:].indirect(
+                    offsets[:, piece * LIST_COLUMNS : (piece + 1) * LIST_COLUMNS]
+                )
+                nc.tensor.matmul(
+                    banks[h][:], w2_mean[:], looked_up, start=False, stop=(t == NEIGHBOURS - 1)
+                )
+            r_half = r[:, h * HALF : (h + 1) * HALF]
+            nc.scalar.activation(r_half, banks[h][:], ACT.Relu, bias=bias[:, 0:1])
+            nc.vector.bn_stats(stats[:, h * BN_STATS_DIM : (h + 1) * BN_STATS_DIM], r_half)
+
+        mean_var = held.tile([P, 2], F32, name="mean_var")
+        nc.vector.bn_aggr(mean_var[:], stats[:])
+        std = held.tile([P, 1], F32, name="std")
+        nc.scalar.activation(std[:], mean_var[:, 1:2], ACT.Sqrt, bias=eps[:, 0:1])
+        rstd = held.tile([P, 1], F32, name="rstd")
+        nc.vector.reciprocal(rstd[:], std[:])
+        slope = held.tile([P, 1], F32, name="slope")
+        nc.vector.tensor_mul(slope[:], gain_sb[:], rstd[:])
+        mean_slope = held.tile([P, 1], F32, name="mean_slope")
+        nc.vector.tensor_mul(mean_slope[:], mean_var[:, 0:1], slope[:])
+        offset = held.tile([P, 1], F32, name="offset")
+        nc.vector.tensor_sub(offset[:], shift_sb[:], mean_slope[:])
+
+        y = held.tile([P, NODES], F32, name="y")
+        nc.vector.tensor_scalar(
+            y[:, 0:HALF], r[:, 0:HALF], slope[:, 0:1], offset[:, 0:1], op0=ALU.mult, op1=ALU.add
+        )
+        nc.sync.dma_start(out[:, 0:HALF], y[:, 0:HALF])
+        nc.scalar.activation(
+            y[:, HALF:NODES], r[:, HALF:NODES], ACT.Identity, bias=offset[:, 0:1], scale=slope[:, 0:1]
+        )
+        nc.scalar.dma_start(out[:, HALF:NODES], y[:, HALF:NODES])

@@ -45,6 +45,8 @@ def tile_resgcnnet_kernel(tc, x, w1, b1, w2, b2, gain, shift, offs, out):
         nc.vector.tensor_add(bias[:], b1_sb[:], b2_sb[:])
         eps = held.tile([P, 1], F32, name="eps")
         nc.vector.memset(eps[:], EPS)
+        table_warm = held.tile([P, 1], F32, name="table_warm")
+        nc.scalar.activation(table_warm[:], eps[:], ACT.Sqrt)
 
         banks = [psum.tile([P, HALF], F32, name=f"bank{h}") for h in range(HALVES)]
         for h in range(HALVES):

@@ -11,6 +11,7 @@ HALF = 512
 HALVES = NODES // HALF
 LIST_COLUMNS = HALF // 16
 EPS = 1e-5
+WARM_MATMULS = 6
 BN_STATS_DIM = 6
 
 FLOPS = 2 * P * P * NODES * (1 + NEIGHBOURS)
@@ -22,6 +23,12 @@ def tile_resgcnnet_kernel(tc, x, w1, b1, w2, b2, gain, shift, offs, out):
         tc.tile_pool(name="held", bufs=1) as held,
         tc.psum_pool(name="psum", bufs=1) as psum,
     ):
+        zeros = held.tile([P, HALF], BF16, name="zeros")
+        nc.vector.memset(zeros[:], 0.0)
+        warm_bank = psum.tile([P, HALF], F32, name="warm_bank")
+        for i in range(WARM_MATMULS):
+            nc.tensor.matmul(warm_bank[:], zeros[:, 0:P], zeros[:], start=True, stop=True)
+
         offsets = held.tile([P, NEIGHBOURS * NODES // 16], U16, name="offsets")
         nc.sync.dma_start(offsets[:], offs)
         nodes = held.tile([P, NODES], BF16, name="nodes")

@@ -53,7 +53,9 @@ def tile_resgcnnet_kernel(tc, x, w1, b1, w2, b2, gain, shift, offs, out):
         eps = held.tile([P, 1], F32, name="eps")
         nc.vector.memset(eps[:], EPS)
         table_warm = held.tile([P, 1], F32, name="table_warm")
-        nc.scalar.activation(table_warm[:], eps[:], ACT.Sqrt)
+        nc.scalar.activation(table_warm[:], eps[:], ACT.Abs_reciprocal_sqrt)
+        neg_gain = held.tile([P, 1], F32, name="neg_gain")
+        nc.vector.tensor_scalar_mul(neg_gain[:], gain_sb[:], -1.0)
 
         banks = [psum.tile([P, HALF], F32, name=f"bank{h}") for h in range(HALVES)]
         for h in range(HALVES):
@@ -78,16 +80,16 @@ def tile_resgcnnet_kernel(tc, x, w1, b1, w2, b2, gain, shift, offs, out):
 
         mean_var = held.tile([P, 2], F32, name="mean_var")
         nc.vector.bn_aggr(mean_var[:], stats[:])
-        std = held.tile([P, 1], F32, name="std")
-        nc.scalar.activation(std[:], mean_var[:, 1:2], ACT.Sqrt, bias=eps[:, 0:1])
         rstd = held.tile([P, 1], F32, name="rstd")
-        nc.vector.reciprocal(rstd[:], std[:])
+        nc.scalar.activation(rstd[:], mean_var[:, 1:2], ACT.Abs_reciprocal_sqrt, bias=eps[:, 0:1])
+        neg_mean_gain = held.tile([P, 1], F32, name="neg_mean_gain")
+        nc.vector.tensor_mul(neg_mean_gain[:], mean_var[:, 0:1], neg_gain[:])
         slope = held.tile([P, 1], F32, name="slope")
         nc.vector.tensor_mul(slope[:], gain_sb[:], rstd[:])
-        mean_slope = held.tile([P, 1], F32, name="mean_slope")
-        nc.vector.tensor_mul(mean_slope[:], mean_var[:, 0:1], slope[:])
         offset = held.tile([P, 1], F32, name="offset")
-        nc.vector.tensor_sub(offset[:], shift_sb[:], mean_slope[:])
+        nc.vector.tensor_scalar(
+            offset[:], neg_mean_gain[:], rstd[:, 0:1], shift_sb[:, 0:1], op0=ALU.mult, op1=ALU.add
+        )
 
         y = held.tile([P, NODES], F32, name="y")
         nc.vector.tensor_scalar(

@@ -9,9 +9,11 @@ NODES = 1024
 NEIGHBOURS = 8
 HALF = 512
 HALVES = NODES // HALF
+QUARTER = 256
+QUARTERS_IN_HALF = HALF // QUARTER
 LIST_COLUMNS = HALF // 16
 EPS = 1e-5
-WARM_MATMULS = 6
+WARM_MATMULS = 4
 BN_STATS_DIM = 6
 
 FLOPS = 2 * P * P * NODES * (1 + NEIGHBOURS)
@@ -64,7 +66,7 @@ def tile_resgcnnet_kernel(tc, x, w1, b1, w2, b2, gain, shift, offs, out):
             )
 
         r = held.tile([P, NODES], F32, name="r")
-        stats = held.tile([P, HALVES * BN_STATS_DIM], F32, name="stats")
+        stats = held.tile([P, (NODES // QUARTER) * BN_STATS_DIM], F32, name="stats")
         for h in range(HALVES):
             for t in range(NEIGHBOURS):
                 piece = HALVES * t + h
@@ -74,9 +76,11 @@ def tile_resgcnnet_kernel(tc, x, w1, b1, w2, b2, gain, shift, offs, out):
                 nc.tensor.matmul(
                     banks[h][:], w2_mean[:], looked_up, start=False, stop=(t == NEIGHBOURS - 1)
                 )
-            r_half = r[:, h * HALF : (h + 1) * HALF]
-            nc.scalar.activation(r_half, banks[h][:], ACT.Relu, bias=bias[:, 0:1])
-            nc.vector.bn_stats(stats[:, h * BN_STATS_DIM : (h + 1) * BN_STATS_DIM], r_half)
+            for q in range(QUARTERS_IN_HALF * h, QUARTERS_IN_HALF * (h + 1)):
+                r_quarter = r[:, q * QUARTER : (q + 1) * QUARTER]
+                z_quarter = banks[h][:, q * QUARTER - h * HALF : (q + 1) * QUARTER - h * HALF]
+                nc.scalar.activation(r_quarter, z_quarter, ACT.Relu, bias=bias[:, 0:1])
+                nc.vector.bn_stats(stats[:, q * BN_STATS_DIM : (q + 1) * BN_STATS_DIM], r_quarter)
 
         mean_var = held.tile([P, 2], F32, name="mean_var")
         nc.vector.bn_aggr(mean_var[:], stats[:])

@@ -11,6 +11,7 @@ HALF = 512
 HALVES = NODES // HALF
 QUARTER = 256
 QUARTERS_IN_HALF = HALF // QUARTER
+VECTOR_QUARTERS = 3
 LIST_COLUMNS = HALF // 16
 EPS = 1e-5
 WARM_MATMULS = 4
@@ -31,14 +32,15 @@ def tile_resgcnnet_kernel(tc, x, w1, b1, w2, b2, gain, shift, offs, out):
         for i in range(WARM_MATMULS):
             nc.tensor.matmul(warm_bank[:], zeros[:, 0:P], zeros[:], start=True, stop=True)
 
-        offsets = held.tile([P, NEIGHBOURS * NODES // 16], U16, name="offsets")
-        nc.sync.dma_start(offsets[:], offs)
-        nodes = held.tile([P, NODES], BF16, name="nodes")
-        nc.scalar.dma_start(nodes[:], x)
         w1_sb = held.tile([P, P], BF16, name="w1_sb")
         nc.scalar.dma_start(w1_sb[:], w1)
         w2_sb = held.tile([P, P], BF16, name="w2_sb")
         nc.sync.dma_start(w2_sb[:], w2)
+        nodes = held.tile([P, NODES], BF16, name="nodes")
+        for h in range(HALVES):
+            nc.scalar.dma_start(nodes[:, h * HALF : (h + 1) * HALF], x[:, h * HALF : (h + 1) * HALF])
+        offsets = held.tile([P, NEIGHBOURS * NODES // 16], U16, name="offsets")
+        nc.sync.dma_start(offsets[:], offs)
         b1_sb = held.tile([P, 1], F32, name="b1_sb")
         nc.sync.dma_start(b1_sb[:], b1)
         b2_sb = held.tile([P, 1], F32, name="b2_sb")
@@ -96,11 +98,15 @@ def tile_resgcnnet_kernel(tc, x, w1, b1, w2, b2, gain, shift, offs, out):
         )
 
         y = held.tile([P, NODES], F32, name="y")
-        nc.vector.tensor_scalar(
-            y[:, 0:HALF], r[:, 0:HALF], slope[:, 0:1], offset[:, 0:1], op0=ALU.mult, op1=ALU.add
-        )
-        nc.sync.dma_start(out[:, 0:HALF], y[:, 0:HALF])
-        nc.scalar.activation(
-            y[:, HALF:NODES], r[:, HALF:NODES], ACT.Identity, bias=offset[:, 0:1], scale=slope[:, 0:1]
-        )
-        nc.scalar.dma_start(out[:, HALF:NODES], y[:, HALF:NODES])
+        for q in range(VECTOR_QUARTERS):
+            columns = slice(q * QUARTER, (q + 1) * QUARTER)
+            nc.vector.tensor_scalar(
+                y[:, columns], r[:, columns], slope[:, 0:1], offset[:, 0:1], op0=ALU.mult, op1=ALU.add
+            )
+            nc.sync.dma_start(out[:, columns], y[:, columns])
+        for q in range(VECTOR_QUARTERS, NODES // QUARTER):
+            columns = slice(q * QUARTER, (q + 1) * QUARTER)
+            nc.scalar.activation(
+                y[:, columns], r[:, columns], ACT.Identity, bias=offset[:, 0:1], scale=slope[:, 0:1]
+            )
+            nc.scalar.dma_start(out[:, columns], y[:, columns])

@@ -41,23 +41,24 @@ def tile_resgcnnet_kernel(tc, x, w1, b1, w2, b2, gain, shift, offs, out):
             nc.scalar.dma_start(nodes[:, h * HALF : (h + 1) * HALF], x[:, h * HALF : (h + 1) * HALF])
         offsets = held.tile([P, NEIGHBOURS * NODES // 16], U16, name="offsets")
         nc.sync.dma_start(offsets[:], offs)
-        b1_sb = held.tile([P, 1], F32, name="b1_sb")
-        nc.sync.dma_start(b1_sb[:], b1)
-        b2_sb = held.tile([P, 1], F32, name="b2_sb")
-        nc.sync.dma_start(b2_sb[:], b2)
-        gain_sb = held.tile([P, 1], F32, name="gain_sb")
-        nc.scalar.dma_start(gain_sb[:], gain)
-        shift_sb = held.tile([P, 1], F32, name="shift_sb")
-        nc.scalar.dma_start(shift_sb[:], shift)
 
         w2_mean = held.tile([P, P], BF16, name="w2_mean")
         nc.vector.tensor_scalar_mul(w2_mean[:], w2_sb[:], 1.0 / NEIGHBOURS)
-        bias = held.tile([P, 1], F32, name="bias")
-        nc.vector.tensor_add(bias[:], b1_sb[:], b2_sb[:])
         eps = held.tile([P, 1], F32, name="eps")
         nc.vector.memset(eps[:], EPS)
         table_warm = held.tile([P, 1], F32, name="table_warm")
         nc.scalar.activation(table_warm[:], eps[:], ACT.Abs_reciprocal_sqrt)
+
+        b1_sb = held.tile([P, 1], F32, name="b1_sb")
+        nc.scalar.dma_start(b1_sb[:], b1)
+        b2_sb = held.tile([P, 1], F32, name="b2_sb")
+        nc.scalar.dma_start(b2_sb[:], b2)
+        gain_sb = held.tile([P, 1], F32, name="gain_sb")
+        nc.scalar.dma_start(gain_sb[:], gain)
+        shift_sb = held.tile([P, 1], F32, name="shift_sb")
+        nc.scalar.dma_start(shift_sb[:], shift)
+        bias = held.tile([P, 1], F32, name="bias")
+        nc.vector.tensor_add(bias[:], b1_sb[:], b2_sb[:])
         neg_gain = held.tile([P, 1], F32, name="neg_gain")
         nc.vector.tensor_scalar_mul(neg_gain[:], gain_sb[:], -1.0)
 

@@ -14,7 +14,7 @@ QUARTERS_IN_HALF = HALF // QUARTER
 VECTOR_QUARTERS = 3
 LIST_COLUMNS = HALF // 16
 EPS = 1e-5
-WARM_MATMULS = 4
+WARM_MATMULS = 12
 BN_STATS_DIM = 6
 
 FLOPS = 2 * P * P * NODES * (1 + NEIGHBOURS)
@@ -26,11 +26,11 @@ def tile_resgcnnet_kernel(tc, x, w1, b1, w2, b2, gain, shift, offs, out):
         tc.tile_pool(name="held", bufs=1) as held,
         tc.psum_pool(name="psum", bufs=1) as psum,
     ):
-        zeros = held.tile([P, HALF], BF16, name="zeros")
+        zeros = held.tile([P, P], BF16, name="zeros")
         nc.vector.memset(zeros[:], 0.0)
-        warm_bank = psum.tile([P, HALF], F32, name="warm_bank")
+        warm_bank = psum.tile([P, P], F32, name="warm_bank")
         for i in range(WARM_MATMULS):
-            nc.tensor.matmul(warm_bank[:], zeros[:, 0:P], zeros[:], start=True, stop=True)
+            nc.tensor.matmul(warm_bank[:], zeros[:], zeros[:], start=True, stop=True)
 
         w1_sb = held.tile([P, P], BF16, name="w1_sb")
         nc.scalar.dma_start(w1_sb[:], w1)

@@ -10,7 +10,7 @@ NEIGHBOURS = 8
 HALF = 512
 HALVES = NODES // HALF
 QUARTER = 256
-QUARTERS_IN_HALF = HALF // QUARTER
+STEPS_IN_HALF = (1, 4)
 VECTOR_QUARTERS = 3
 LIST_COLUMNS = HALF // 16
 EPS = 1e-5
@@ -61,6 +61,11 @@ def tile_resgcnnet_kernel(tc, x, w1, b1, w2, b2, gain, shift, offs, out):
         nc.vector.tensor_add(bias[:], b1_sb[:], b2_sb[:])
         neg_gain = held.tile([P, 1], F32, name="neg_gain")
         nc.vector.tensor_scalar_mul(neg_gain[:], gain_sb[:], -1.0)
+        factors = held.tile([P, 2], F32, name="factors")
+        nc.vector.tensor_copy(factors[:, 0:1], gain_sb[:])
+        addends = held.tile([P, 2], F32, name="addends")
+        nc.vector.memset(addends[:, 0:1], 0.0)
+        nc.vector.tensor_copy(addends[:, 1:2], shift_sb[:])
 
         banks = [psum.tile([P, HALF], F32, name=f"bank{h}") for h in range(HALVES)]
         for h in range(HALVES):
@@ -69,7 +74,7 @@ def tile_resgcnnet_kernel(tc, x, w1, b1, w2, b2, gain, shift, offs, out):
             )
 
         r = held.tile([P, NODES], F32, name="r")
-        stats = held.tile([P, (NODES // QUARTER) * BN_STATS_DIM], F32, name="stats")
+        stats = held.tile([P, sum(STEPS_IN_HALF) * BN_STATS_DIM], F32, name="stats")
         for h in range(HALVES):
             for t in range(NEIGHBOURS):
                 piece = HALVES * t + h
@@ -79,35 +84,36 @@ def tile_resgcnnet_kernel(tc, x, w1, b1, w2, b2, gain, shift, offs, out):
                 nc.tensor.matmul(
                     banks[h][:], w2_mean[:], looked_up, start=False, stop=(t == NEIGHBOURS - 1)
                 )
-            for q in range(QUARTERS_IN_HALF * h, QUARTERS_IN_HALF * (h + 1)):
-                r_quarter = r[:, q * QUARTER : (q + 1) * QUARTER]
-                z_quarter = banks[h][:, q * QUARTER - h * HALF : (q + 1) * QUARTER - h * HALF]
-                nc.scalar.activation(r_quarter, z_quarter, ACT.Relu, bias=bias[:, 0:1])
-                nc.vector.bn_stats(stats[:, q * BN_STATS_DIM : (q + 1) * BN_STATS_DIM], r_quarter)
+            step = HALF // STEPS_IN_HALF[h]
+            for s in range(STEPS_IN_HALF[h]):
+                z_step = banks[h][:, s * step : (s + 1) * step]
+                r_step = r[:, h * HALF + s * step : h * HALF + (s + 1) * step]
+                nc.scalar.activation(r_step, z_step, ACT.Relu, bias=bias[:, 0:1])
+                k = sum(STEPS_IN_HALF[:h]) + s
+                nc.vector.bn_stats(stats[:, k * BN_STATS_DIM : (k + 1) * BN_STATS_DIM], r_step)
 
         mean_var = held.tile([P, 2], F32, name="mean_var")
         nc.vector.bn_aggr(mean_var[:], stats[:])
         rstd = held.tile([P, 1], F32, name="rstd")
         nc.scalar.activation(rstd[:], mean_var[:, 1:2], ACT.Abs_reciprocal_sqrt, bias=eps[:, 0:1])
-        neg_mean_gain = held.tile([P, 1], F32, name="neg_mean_gain")
-        nc.vector.tensor_mul(neg_mean_gain[:], mean_var[:, 0:1], neg_gain[:])
-        slope = held.tile([P, 1], F32, name="slope")
-        nc.vector.tensor_mul(slope[:], gain_sb[:], rstd[:])
-        offset = held.tile([P, 1], F32, name="offset")
-        nc.vector.tensor_scalar(
-            offset[:], neg_mean_gain[:], rstd[:, 0:1], shift_sb[:, 0:1], op0=ALU.mult, op1=ALU.add
+        nc.vector.tensor_mul(factors[:, 1:2], mean_var[:, 0:1], neg_gain[:])
+        slope_offset = held.tile([P, 2], F32, name="slope_offset")
+        nc.vector.scalar_tensor_tensor(
+            slope_offset[:], factors[:], rstd[:, 0:1], addends[:], op0=ALU.mult, op1=ALU.add
         )
+        slope = slope_offset[:, 0:1]
+        offset = slope_offset[:, 1:2]
 
         y = held.tile([P, NODES], F32, name="y")
         for q in range(VECTOR_QUARTERS):
             columns = slice(q * QUARTER, (q + 1) * QUARTER)
             nc.vector.tensor_scalar(
-                y[:, columns], r[:, columns], slope[:, 0:1], offset[:, 0:1], op0=ALU.mult, op1=ALU.add
+                y[:, columns], r[:, columns], slope, offset, op0=ALU.mult, op1=ALU.add
             )
             nc.sync.dma_start(out[:, columns], y[:, columns])
         for q in range(VECTOR_QUARTERS, NODES // QUARTER):
             columns = slice(q * QUARTER, (q + 1) * QUARTER)
             nc.scalar.activation(
-                y[:, columns], r[:, columns], ACT.Identity, bias=offset[:, 0:1], scale=slope[:, 0:1]
+                y[:, columns], r[:, columns], ACT.Identity, bias=offset, scale=slope
             )
             nc.scalar.dma_start(out[:, columns], y[:, columns])

@@ -10,8 +10,8 @@ NEIGHBOURS = 8
 HALF = 512
 HALVES = NODES // HALF
 QUARTER = 256
+CENTRED_QUARTERS = 2
 STEPS_IN_HALF = (1, 4)
-VECTOR_QUARTERS = 3
 LIST_COLUMNS = HALF // 16
 EPS = 1e-5
 WARM_MATMULS = 12
@@ -97,23 +97,31 @@ def tile_resgcnnet_kernel(tc, x, w1, b1, w2, b2, gain, shift, offs, out):
         rstd = held.tile([P, 1], F32, name="rstd")
         nc.scalar.activation(rstd[:], mean_var[:, 1:2], ACT.Abs_reciprocal_sqrt, bias=eps[:, 0:1])
         nc.vector.tensor_mul(factors[:, 1:2], mean_var[:, 0:1], neg_gain[:])
-        slope_offset = held.tile([P, 2], F32, name="slope_offset")
-        nc.vector.scalar_tensor_tensor(
-            slope_offset[:], factors[:], rstd[:, 0:1], addends[:], op0=ALU.mult, op1=ALU.add
-        )
-        slope = slope_offset[:, 0:1]
-        offset = slope_offset[:, 1:2]
-
-        y = held.tile([P, NODES], F32, name="y")
-        for q in range(VECTOR_QUARTERS):
+        centred = held.tile([P, CENTRED_QUARTERS * QUARTER], F32, name="centred")
+        for q in range(CENTRED_QUARTERS):
             columns = slice(q * QUARTER, (q + 1) * QUARTER)
             nc.vector.tensor_scalar(
-                y[:, columns], r[:, columns], slope, offset, op0=ALU.mult, op1=ALU.add
+                centred[:, columns], r[:, columns], mean_var[:, 0:1], gain_sb[:, 0:1],
+                op0=ALU.subtract, op1=ALU.mult,
             )
-            nc.sync.dma_start(out[:, columns], y[:, columns])
-        for q in range(VECTOR_QUARTERS, NODES // QUARTER):
+
+        y = held.tile([P, NODES], F32, name="y")
+        slope_offset = held.tile([P, 2], F32, name="slope_offset")
+        for q in range(NODES // QUARTER):
             columns = slice(q * QUARTER, (q + 1) * QUARTER)
-            nc.scalar.activation(
-                y[:, columns], r[:, columns], ACT.Identity, bias=offset, scale=slope
-            )
-            nc.scalar.dma_start(out[:, columns], y[:, columns])
+            if q < CENTRED_QUARTERS:
+                nc.vector.tensor_scalar(
+                    y[:, columns], centred[:, columns], rstd[:, 0:1], shift_sb[:, 0:1],
+                    op0=ALU.mult, op1=ALU.add,
+                )
+            else:
+                nc.vector.tensor_scalar(
+                    y[:, columns], r[:, columns], slope_offset[:, 0:1], slope_offset[:, 1:2],
+                    op0=ALU.mult, op1=ALU.add,
+                )
+            queue = nc.sync if q % 2 == 0 else nc.scalar
+            queue.dma_start(out[:, columns], y[:, columns])
+            if q == 0:
+                nc.vector.scalar_tensor_tensor(
+                    slope_offset[:], factors[:], rstd[:, 0:1], addends[:], op0=ALU.mult, op1=ALU.add
+                )

@@ -34,16 +34,16 @@ def tile_resgcnnet_kernel(tc, x, w1, b1, w2, b2, gain, shift, offs, out):
 
         w1_sb = held.tile([P, P], BF16, name="w1_sb")
         nc.scalar.dma_start(w1_sb[:], w1)
-        w2_sb = held.tile([P, P], BF16, name="w2_sb")
-        nc.sync.dma_start(w2_sb[:], w2)
         nodes = held.tile([P, NODES], BF16, name="nodes")
-        for h in range(HALVES):
-            nc.scalar.dma_start(nodes[:, h * HALF : (h + 1) * HALF], x[:, h * HALF : (h + 1) * HALF])
+        nc.sync.dma_start(nodes[:, HALF:NODES], x[:, HALF:NODES])
+        nc.scalar.dma_start(nodes[:, 0:HALF], x[:, 0:HALF])
         offsets = held.tile([P, NEIGHBOURS * NODES // 16], U16, name="offsets")
         nc.sync.dma_start(offsets[:], offs)
+        w2_sb = held.tile([P, P], BF16, name="w2_sb")
+        nc.scalar.dma_start(w2_sb[:], w2)
 
-        w2_mean = held.tile([P, P], BF16, name="w2_mean")
-        nc.vector.tensor_scalar_mul(w2_mean[:], w2_sb[:], 1.0 / NEIGHBOURS)
+        w1_times_8 = held.tile([P, P], BF16, name="w1_times_8")
+        nc.vector.tensor_scalar_mul(w1_times_8[:], w1_sb[:], float(NEIGHBOURS))
         eps = held.tile([P, 1], F32, name="eps")
         nc.vector.memset(eps[:], EPS)
         table_warm = held.tile([P, 1], F32, name="table_warm")
@@ -68,9 +68,9 @@ def tile_resgcnnet_kernel(tc, x, w1, b1, w2, b2, gain, shift, offs, out):
         nc.vector.tensor_copy(addends[:, 1:2], shift_sb[:])
 
         banks = [psum.tile([P, HALF], F32, name=f"bank{h}") for h in range(HALVES)]
-        for h in range(HALVES):
+        for h in reversed(range(HALVES)):
             nc.tensor.matmul(
-                banks[h][:], w1_sb[:], nodes[:, h * HALF : (h + 1) * HALF], start=True, stop=False
+                banks[h][:], w1_times_8[:], nodes[:, h * HALF : (h + 1) * HALF], start=True, stop=False
             )
 
         r = held.tile([P, NODES], F32, name="r")
@@ -82,13 +82,13 @@ def tile_resgcnnet_kernel(tc, x, w1, b1, w2, b2, gain, shift, offs, out):
                     offsets[:, piece * LIST_COLUMNS : (piece + 1) * LIST_COLUMNS]
                 )
                 nc.tensor.matmul(
-                    banks[h][:], w2_mean[:], looked_up, start=False, stop=(t == NEIGHBOURS - 1)
+                    banks[h][:], w2_sb[:], looked_up, start=False, stop=(t == NEIGHBOURS - 1)
                 )
             step = HALF // STEPS_IN_HALF[h]
             for s in range(STEPS_IN_HALF[h]):
                 z_step = banks[h][:, s * step : (s + 1) * step]
                 r_step = r[:, h * HALF + s * step : h * HALF + (s + 1) * step]
-                nc.scalar.activation(r_step, z_step, ACT.Relu, bias=bias[:, 0:1])
+                nc.scalar.activation(r_step, z_step, ACT.Relu, bias=bias[:, 0:1], scale=1.0 / NEIGHBOURS)
                 k = sum(STEPS_IN_HALF[:h]) + s
                 nc.vector.bn_stats(stats[:, k * BN_STATS_DIM : (k + 1) * BN_STATS_DIM], r_step)
 

@@ -9,12 +9,12 @@ NODES = 1024
 NEIGHBOURS = 8
 HALF = 512
 HALVES = NODES // HALF
-QUARTER = 256
-CENTRED_QUARTERS = 2
+PIECES = ((0, 128), (128, 256), (256, 512), (512, 1024))
+CENTRED = 512
 STEPS_IN_HALF = (1, 4)
 LIST_COLUMNS = HALF // 16
 EPS = 1e-5
-WARM_MATMULS = 12
+WARM_MATMULS = 4
 BN_STATS_DIM = 6
 
 FLOPS = 2 * P * P * NODES * (1 + NEIGHBOURS)
@@ -26,11 +26,13 @@ def tile_resgcnnet_kernel(tc, x, w1, b1, w2, b2, gain, shift, offs, out):
         tc.tile_pool(name="held", bufs=1) as held,
         tc.psum_pool(name="psum", bufs=1) as psum,
     ):
-        zeros = held.tile([P, P], BF16, name="zeros")
-        nc.vector.memset(zeros[:], 0.0)
-        warm_bank = psum.tile([P, P], F32, name="warm_bank")
+        zeros = held.tile([P, 2], BF16, name="zeros")
+        nc.gpsimd.memset(zeros[:], 0.0)
+        zero_weights = zeros[:, 0:1].to_broadcast([P, P])
+        zero_columns = zeros[:, 0:1].to_broadcast([P, HALF])
+        warm_bank = psum.tile([P, HALF], F32, name="warm_bank")
         for i in range(WARM_MATMULS):
-            nc.tensor.matmul(warm_bank[:], zeros[:], zeros[:], start=True, stop=True)
+            nc.tensor.matmul(warm_bank[:], zero_weights, zero_columns, start=True, stop=True)
 
         w1_sb = held.tile([P, P], BF16, name="w1_sb")
         nc.scalar.dma_start(w1_sb[:], w1)
@@ -97,31 +99,30 @@ def tile_resgcnnet_kernel(tc, x, w1, b1, w2, b2, gain, shift, offs, out):
         rstd = held.tile([P, 1], F32, name="rstd")
         nc.scalar.activation(rstd[:], mean_var[:, 1:2], ACT.Abs_reciprocal_sqrt, bias=eps[:, 0:1])
         nc.vector.tensor_mul(factors[:, 1:2], mean_var[:, 0:1], neg_gain[:])
-        centred = held.tile([P, CENTRED_QUARTERS * QUARTER], F32, name="centred")
-        for q in range(CENTRED_QUARTERS):
-            columns = slice(q * QUARTER, (q + 1) * QUARTER)
-            nc.vector.tensor_scalar(
-                centred[:, columns], r[:, columns], mean_var[:, 0:1], gain_sb[:, 0:1],
-                op0=ALU.subtract, op1=ALU.mult,
-            )
+        centred = held.tile([P, CENTRED], F32, name="centred")
+        for start, stop in PIECES:
+            if stop <= CENTRED:
+                nc.vector.tensor_scalar(
+                    centred[:, start:stop], r[:, start:stop], mean_var[:, 0:1], gain_sb[:, 0:1],
+                    op0=ALU.subtract, op1=ALU.mult,
+                )
 
         y = held.tile([P, NODES], F32, name="y")
         slope_offset = held.tile([P, 2], F32, name="slope_offset")
-        for q in range(NODES // QUARTER):
-            columns = slice(q * QUARTER, (q + 1) * QUARTER)
-            if q < CENTRED_QUARTERS:
+        for i, (start, stop) in enumerate(PIECES):
+            if stop <= CENTRED:
                 nc.vector.tensor_scalar(
-                    y[:, columns], centred[:, columns], rstd[:, 0:1], shift_sb[:, 0:1],
+                    y[:, start:stop], centred[:, start:stop], rstd[:, 0:1], shift_sb[:, 0:1],
                     op0=ALU.mult, op1=ALU.add,
                 )
             else:
                 nc.vector.tensor_scalar(
-                    y[:, columns], r[:, columns], slope_offset[:, 0:1], slope_offset[:, 1:2],
+                    y[:, start:stop], r[:, start:stop], slope_offset[:, 0:1], slope_offset[:, 1:2],
                     op0=ALU.mult, op1=ALU.add,
                 )
-            queue = nc.sync if q % 2 == 0 else nc.scalar
-            queue.dma_start(out[:, columns], y[:, columns])
-            if q == 0:
+            queue = nc.sync if i % 2 == 0 else nc.scalar
+            queue.dma_start(out[:, start:stop], y[:, start:stop])
+            if i == 0:
                 nc.vector.scalar_tensor_tensor(
                     slope_offset[:], factors[:], rstd[:, 0:1], addends[:], op0=ALU.mult, op1=ALU.add
                 )

@@ -15,6 +15,7 @@ STEPS_IN_HALF = (1, 4)
 LIST_COLUMNS = HALF // 16
 EPS = 1e-5
 WARM_MATMULS = 4
+BLOCK = 8
 BN_STATS_DIM = 6
 
 FLOPS = 2 * P * P * NODES * (1 + NEIGHBOURS)
@@ -51,29 +52,25 @@ def tile_resgcnnet_kernel(tc, x, w1, b1, w2, b2, gain, shift, offs, out):
         table_warm = held.tile([P, 1], F32, name="table_warm")
         nc.scalar.activation(table_warm[:], eps[:], ACT.Abs_reciprocal_sqrt)
 
-        b1_sb = held.tile([P, 1], F32, name="b1_sb")
-        nc.scalar.dma_start(b1_sb[:], b1)
-        b2_sb = held.tile([P, 1], F32, name="b2_sb")
-        nc.scalar.dma_start(b2_sb[:], b2)
-        gain_sb = held.tile([P, 1], F32, name="gain_sb")
-        nc.scalar.dma_start(gain_sb[:], gain)
-        shift_sb = held.tile([P, 1], F32, name="shift_sb")
-        nc.scalar.dma_start(shift_sb[:], shift)
-        bias = held.tile([P, 1], F32, name="bias")
-        nc.vector.tensor_add(bias[:], b1_sb[:], b2_sb[:])
-        neg_gain = held.tile([P, 1], F32, name="neg_gain")
-        nc.vector.tensor_scalar_mul(neg_gain[:], gain_sb[:], -1.0)
-        factors = held.tile([P, 2], F32, name="factors")
-        nc.vector.tensor_copy(factors[:, 0:1], gain_sb[:])
-        addends = held.tile([P, 2], F32, name="addends")
-        nc.vector.memset(addends[:, 0:1], 0.0)
-        nc.vector.tensor_copy(addends[:, 1:2], shift_sb[:])
-
         banks = [psum.tile([P, HALF], F32, name=f"bank{h}") for h in range(HALVES)]
         for h in reversed(range(HALVES)):
             nc.tensor.matmul(
                 banks[h][:], w1_times_8[:], nodes[:, h * HALF : (h + 1) * HALF], start=True, stop=False
             )
+
+        vectors = held.tile([P, 4 * BLOCK], F32, name="vectors", tag="w1_times_8")
+        b1_sb, b2_sb, gain_sb, shift_sb = [vectors[:, i * BLOCK : i * BLOCK + 1] for i in range(4)]
+        for column, vector in ((b1_sb, b1), (b2_sb, b2), (gain_sb, gain), (shift_sb, shift)):
+            nc.scalar.dma_start(column, vector)
+        bias = held.tile([P, 1], F32, name="bias")
+        nc.vector.tensor_add(bias[:], b1_sb, b2_sb)
+        neg_gain = held.tile([P, 1], F32, name="neg_gain")
+        nc.vector.tensor_scalar_mul(neg_gain[:], gain_sb, -1.0)
+        factors = held.tile([P, 2], F32, name="factors")
+        nc.vector.tensor_copy(factors[:, 0:1], gain_sb)
+        addends = held.tile([P, 2], F32, name="addends")
+        nc.vector.memset(addends[:, 0:1], 0.0)
+        nc.vector.tensor_copy(addends[:, 1:2], shift_sb)
 
         r = held.tile([P, NODES], F32, name="r")
         stats = held.tile([P, sum(STEPS_IN_HALF) * BN_STATS_DIM], F32, name="stats")
@@ -103,7 +100,7 @@ def tile_resgcnnet_kernel(tc, x, w1, b1, w2, b2, gain, shift, offs, out):
         for start, stop in PIECES:
             if stop <= CENTRED:
                 nc.vector.tensor_scalar(
-                    centred[:, start:stop], r[:, start:stop], mean_var[:, 0:1], gain_sb[:, 0:1],
+                    centred[:, start:stop], r[:, start:stop], mean_var[:, 0:1], gain_sb,
                     op0=ALU.subtract, op1=ALU.mult,
                 )
 
@@ -112,7 +109,7 @@ def tile_resgcnnet_kernel(tc, x, w1, b1, w2, b2, gain, shift, offs, out):
         for i, (start, stop) in enumerate(PIECES):
             if stop <= CENTRED:
                 nc.vector.tensor_scalar(
-                    y[:, start:stop], centred[:, start:stop], rstd[:, 0:1], shift_sb[:, 0:1],
+                    y[:, start:stop], centred[:, start:stop], rstd[:, 0:1], shift_sb,
                     op0=ALU.mult, op1=ALU.add,
                 )
             else:

@@ -36,10 +36,10 @@ def tile_resgcnnet_kernel(tc, x, w1, b1, w2, b2, gain, shift, offs, out):
             nc.tensor.matmul(warm_bank[:], zero_weights, zero_columns, start=True, stop=True)
 
         w1_sb = held.tile([P, P], BF16, name="w1_sb")
-        nc.scalar.dma_start(w1_sb[:], w1)
+        nc.sync.dma_start(w1_sb[:], w1)
         nodes = held.tile([P, NODES], BF16, name="nodes")
-        nc.sync.dma_start(nodes[:, HALF:NODES], x[:, HALF:NODES])
-        nc.scalar.dma_start(nodes[:, 0:HALF], x[:, 0:HALF])
+        for h in range(HALVES):
+            nc.scalar.dma_start(nodes[:, h * HALF : (h + 1) * HALF], x[:, h * HALF : (h + 1) * HALF])
         offsets = held.tile([P, NEIGHBOURS * NODES // 16], U16, name="offsets")
         nc.sync.dma_start(offsets[:], offs)
         w2_sb = held.tile([P, P], BF16, name="w2_sb")
@@ -53,7 +53,7 @@ def tile_resgcnnet_kernel(tc, x, w1, b1, w2, b2, gain, shift, offs, out):
         nc.scalar.activation(table_warm[:], eps[:], ACT.Abs_reciprocal_sqrt)
 
         banks = [psum.tile([P, HALF], F32, name=f"bank{h}") for h in range(HALVES)]
-        for h in reversed(range(HALVES)):
+        for h in range(HALVES):
             nc.tensor.matmul(
                 banks[h][:], w1_times_8[:], nodes[:, h * HALF : (h + 1) * HALF], start=True, stop=False
             )

import concourse.mybir as mybir

BF16, F32, U16 = mybir.dt.bfloat16, mybir.dt.float32, mybir.dt.uint16
ACT = mybir.ActivationFunctionType
ALU = mybir.AluOpType

P = 128
NODES = 1024
NEIGHBOURS = 8
HALF = 512
HALVES = NODES // HALF
PIECES = ((0, 128), (128, 256), (256, 512), (512, 1024))
CENTRED = 512
STEPS_IN_HALF = (1, 4)
LIST_COLUMNS = HALF // 16
EPS = 1e-5
WARM_MATMULS = 4
BLOCK = 8
BN_STATS_DIM = 6

FLOPS = 2 * P * P * NODES * (1 + NEIGHBOURS)


def tile_resgcnnet_kernel(tc, x, w1, b1, w2, b2, gain, shift, offs, out):
    nc = tc.nc
    with (
        tc.tile_pool(name="held", bufs=1) as held,
        tc.psum_pool(name="psum", bufs=1) as psum,
    ):
        zeros = held.tile([P, 2], BF16, name="zeros")
        nc.gpsimd.memset(zeros[:], 0.0)
        zero_weights = zeros[:, 0:1].to_broadcast([P, P])
        zero_columns = zeros[:, 0:1].to_broadcast([P, HALF])
        warm_bank = psum.tile([P, HALF], F32, name="warm_bank")
        for i in range(WARM_MATMULS):
            nc.tensor.matmul(warm_bank[:], zero_weights, zero_columns, start=True, stop=True)

        w1_sb = held.tile([P, P], BF16, name="w1_sb")
        nc.sync.dma_start(w1_sb[:], w1)
        nodes = held.tile([P, NODES], BF16, name="nodes")
        for h in range(HALVES):
            nc.scalar.dma_start(nodes[:, h * HALF : (h + 1) * HALF], x[:, h * HALF : (h + 1) * HALF])
        offsets = held.tile([P, NEIGHBOURS * NODES // 16], U16, name="offsets")
        nc.sync.dma_start(offsets[:], offs)
        w2_sb = held.tile([P, P], BF16, name="w2_sb")
        nc.scalar.dma_start(w2_sb[:], w2)

        w1_times_8 = held.tile([P, P], BF16, name="w1_times_8")
        nc.vector.tensor_scalar_mul(w1_times_8[:], w1_sb[:], float(NEIGHBOURS))
        eps = held.tile([P, 1], F32, name="eps")
        nc.vector.memset(eps[:], EPS)
        table_warm = held.tile([P, 1], F32, name="table_warm")
        nc.scalar.activation(table_warm[:], eps[:], ACT.Abs_reciprocal_sqrt)

        banks = [psum.tile([P, HALF], F32, name=f"bank{h}") for h in range(HALVES)]
        for h in range(HALVES):
            nc.tensor.matmul(
                banks[h][:], w1_times_8[:], nodes[:, h * HALF : (h + 1) * HALF], start=True, stop=False
            )

        vectors = held.tile([P, 4 * BLOCK], F32, name="vectors", tag="w1_times_8")
        b1_sb, b2_sb, gain_sb, shift_sb = [vectors[:, i * BLOCK : i * BLOCK + 1] for i in range(4)]
        for column, vector in ((b1_sb, b1), (b2_sb, b2), (gain_sb, gain), (shift_sb, shift)):
            nc.scalar.dma_start(column, vector)
        bias = held.tile([P, 1], F32, name="bias")
        nc.vector.tensor_add(bias[:], b1_sb, b2_sb)
        neg_gain = held.tile([P, 1], F32, name="neg_gain")
        nc.vector.tensor_scalar_mul(neg_gain[:], gain_sb, -1.0)
        factors = held.tile([P, 2], F32, name="factors")
        nc.vector.tensor_copy(factors[:, 0:1], gain_sb)
        addends = held.tile([P, 2], F32, name="addends")
        nc.vector.memset(addends[:, 0:1], 0.0)
        nc.vector.tensor_copy(addends[:, 1:2], shift_sb)

        r = held.tile([P, NODES], F32, name="r")
        stats = held.tile([P, sum(STEPS_IN_HALF) * BN_STATS_DIM], F32, name="stats")
        for h in range(HALVES):
            for t in range(NEIGHBOURS):
                piece = HALVES * t + h
                looked_up = nodes[:].indirect(
                    offsets[:, piece * LIST_COLUMNS : (piece + 1) * LIST_COLUMNS]
                )
                nc.tensor.matmul(
                    banks[h][:], w2_sb[:], looked_up, start=False, stop=(t == NEIGHBOURS - 1)
                )
            step = HALF // STEPS_IN_HALF[h]
            for s in range(STEPS_IN_HALF[h]):
                z_step = banks[h][:, s * step : (s + 1) * step]
                r_step = r[:, h * HALF + s * step : h * HALF + (s + 1) * step]
                nc.scalar.activation(r_step, z_step, ACT.Relu, bias=bias[:, 0:1], scale=1.0 / NEIGHBOURS)
                k = sum(STEPS_IN_HALF[:h]) + s
                nc.vector.bn_stats(stats[:, k * BN_STATS_DIM : (k + 1) * BN_STATS_DIM], r_step)

        mean_var = held.tile([P, 2], F32, name="mean_var")
        nc.vector.bn_aggr(mean_var[:], stats[:])
        rstd = held.tile([P, 1], F32, name="rstd")
        nc.scalar.activation(rstd[:], mean_var[:, 1:2], ACT.Abs_reciprocal_sqrt, bias=eps[:, 0:1])
        nc.vector.tensor_mul(factors[:, 1:2], mean_var[:, 0:1], neg_gain[:])
        centred = held.tile([P, CENTRED], F32, name="centred")
        for start, stop in PIECES:
            if stop <= CENTRED:
                nc.vector.tensor_scalar(
                    centred[:, start:stop], r[:, start:stop], mean_var[:, 0:1], gain_sb,
                    op0=ALU.subtract, op1=ALU.mult,
                )

        y = held.tile([P, NODES], F32, name="y")
        slope_offset = held.tile([P, 2], F32, name="slope_offset")
        for i, (start, stop) in enumerate(PIECES):
            if stop <= CENTRED:
                nc.vector.tensor_scalar(
                    y[:, start:stop], centred[:, start:stop], rstd[:, 0:1], shift_sb,
                    op0=ALU.mult, op1=ALU.add,
                )
            else:
                nc.vector.tensor_scalar(
                    y[:, start:stop], r[:, start:stop], slope_offset[:, 0:1], slope_offset[:, 1:2],
                    op0=ALU.mult, op1=ALU.add,
                )
            queue = nc.sync if i % 2 == 0 else nc.scalar
            queue.dma_start(out[:, start:stop], y[:, start:stop])
            if i == 0:
                nc.vector.scalar_tensor_tensor(
                    slope_offset[:], factors[:], rstd[:, 0:1], addends[:], op0=ALU.mult, op1=ALU.add
                )
